import numpy as np
import ml_dtypes

BF16 = ml_dtypes.bfloat16


def bf(x):
    return np.asarray(x, np.float32).astype(BF16)


def f32(x):
    return np.asarray(x, np.float32)


def f64(x):
    return np.asarray(x).astype(np.float64)


def striped(idx):
    return np.tile(idx.reshape(-1, 16).T, (8, 1))


H, W, C, S, N, XY, CH = 16, 32, 512, 256, 128, 2, 3
CHOL_LO = np.array([[3.0], [-2.0], [3.0]])
CHOL_BIAS = np.array([[0.5], [0.0], [0.5]])


def setup_inputs():
    u = np.random.uniform(0.01, 0.99, (XY, N))
    return {
        "base": f32(np.random.random((C, S))),
        "xyz_raw": f32(np.arctanh(2.0 * (u - 0.5))),
        "cholesky_raw": f32(CHOL_LO + 4.0 * np.random.random((CH, N))),
        "opacity": f32(1.0 + 0.1 * np.random.standard_normal((1, N))),
        "px": f32(np.tile(np.arange(W), H).reshape(C, 1)),
        "py": f32(np.repeat(np.arange(H), W).reshape(C, 1)),
        "offs": striped(np.random.permutation(S)[:N]),
    }


def reference(base, xyz_raw, cholesky_raw, opacity, px, py, offs):
    idx = offs[:16].T.reshape(-1)
    xy = np.tanh(f64(xyz_raw))
    chol = f64(cholesky_raw) + CHOL_BIAS
    l1, l2, l3 = chol[0], chol[1], chol[2]
    va = l1 * l1
    vb = l1 * l2
    vc = l2 * l2 + l3 * l3
    det = va * vc - vb * vb
    q1, q2, q3 = vc / det, -vb / det, va / det
    cx = 0.5 * ((xy[0] + 1.0) * W - 1.0)
    cy = 0.5 * ((xy[1] + 1.0) * H - 1.0)
    dx = cx[None, :] - f64(px)
    dy = cy[None, :] - f64(py)
    sigma = 0.5 * (q1[None, :] * dx * dx + q3[None, :] * dy * dy) + q2[None, :] * dx * dy
    out = f64(base).copy()
    out[:, idx] = f64(opacity) * np.exp(-sigma)
    return out

@@ -1,0 +1,114 @@
+from contextlib import ExitStack
+
+import concourse.masks as masks
+import concourse.mybir as mybir
+
+F32 = mybir.dt.float32
+U16 = mybir.dt.uint16
+ALU = mybir.AluOpType
+ACT = mybir.ActivationFunctionType
+
+P = 128
+IMAGE_W, IMAGE_H = 32, 16
+N_F = 4
+N_U = 2
+K = N_F * N_U * N_F
+STAGE_ROWS = 64
+
+FLOPS = 2 * K * 512 * 128
+
+
+def tile_gaussianbasis_kernel(tc, base, xyz_raw, cholesky_raw, opacity, px, py, offs, out):
+    nc = tc.nc
+    n_pixels, n_slots = base.shape
+    n_gauss = opacity.shape[1]
+    n_blocks = n_pixels // P
+    assert n_gauss == P and n_pixels % P == 0
+
+    with ExitStack() as ctx:
+        held = ctx.enter_context(tc.tile_pool(name="held", bufs=1))
+        psum = ctx.enter_context(tc.psum_pool(name="psum", bufs=1))
+
+        stage = held.tile([STAGE_ROWS, n_gauss], F32)
+        nc.vector.memset(stage[:], 0.0)
+        second = held.tile([K, n_pixels], F32)
+        nc.gpsimd.memset(second[:], 1.0)
+        identity = held.tile([P, P], F32)
+        masks.make_identity(nc, identity[:])
+        first = held.tile([K, n_pixels], F32)
+        ones_rows = 2 * N_U * N_F
+        nc.vector.memset(first[0:ones_rows, :], 1.0)
+        whiten = held.tile([P, N_U, N_F], F32)
+        nc.vector.memset(whiten[:], 0.0)
+
+        nc.sync.dma_start(stage[0:2, :], xyz_raw)
+        nc.scalar.dma_start(stage[2:4, :], cholesky_raw[0:2, :])
+        nc.sync.dma_start(stage[4:5, :], cholesky_raw[2:3, :])
+
+        px_row = px.rearrange("c o -> (c o)")
+        py_row = py.rearrange("c o -> (c o)")
+        rows_per_a = N_U * N_F
+        nc.scalar.dma_start(first[2 * rows_per_a : 3 * rows_per_a, :], px_row.partition_broadcast(rows_per_a))
+        nc.sync.dma_start(first[3 * rows_per_a : 4 * rows_per_a, :], py_row.partition_broadcast(rows_per_a))
+        nc.scalar.dma_start(second[2::N_F, :], px_row.partition_broadcast(K // N_F))
+        nc.sync.dma_start(second[3::N_F, :], py_row.partition_broadcast(K // N_F))
+
+        offsets = held.tile([P, n_gauss // 16], U16)
+        nc.sync.dma_start(offsets[:], offs)
+        opacity_all = held.tile([P, n_gauss], F32)
+        nc.scalar.dma_start(opacity_all[:], opacity.rearrange("o n -> (o n)").partition_broadcast(P))
+
+        windows = [held.tile([P, n_slots], F32, name=f"window{blk}") for blk in range(n_blocks)]
+        for blk in range(n_blocks):
+            queue = nc.sync if blk % 2 == 0 else nc.scalar
+            queue.dma_start(windows[blk][:], base[blk * P : (blk + 1) * P, :])
+
+        pixel_products = held.tile([K, n_pixels], F32)
+        nc.gpsimd.tensor_tensor(pixel_products[:], first[:], second[:], ALU.mult)
+
+        params = psum.tile([P, STAGE_ROWS], F32)
+        nc.tensor.transpose(params[:], stage[:], identity[0:STAGE_ROWS, 0:STAGE_ROWS])
+
+        tanh_xy = held.tile([P, 2], F32)
+        nc.scalar.activation(tanh_xy[:], params[:, 0:2], ACT.Tanh)
+        minus_centre = held.tile([P, 2], F32)
+        for axis, size in enumerate((IMAGE_W, IMAGE_H)):
+            nc.vector.tensor_scalar(
+                minus_centre[:, axis : axis + 1], tanh_xy[:, axis : axis + 1],
+                -0.5 * size, -0.5 * (size - 1), ALU.mult, ALU.add,
+            )
+
+        whiten_flat = whiten[:].rearrange("g r a -> g (r a)")
+        minus_l = held.tile([P, 2], F32)
+        nc.vector.tensor_scalar(minus_l[:], params[:, 2:5:2], 0.5, -1.0, ALU.add, ALU.mult)
+        nc.vector.reciprocal(whiten_flat[:, 2 : 2 * N_F : N_F + 1], minus_l[:])
+        nc.vector.tensor_scalar(
+            whiten_flat[:, N_F + 2 : N_F + 3], params[:, 3:4],
+            whiten_flat[:, 2:3], whiten_flat[:, N_F + 3 : N_F + 4], ALU.mult, ALU.mult,
+        )
+        nc.vector.tensor_tensor(
+            whiten[:, :, 0:2], whiten[:, :, 2:4],
+            minus_centre[:].unsqueeze(1).to_broadcast([P, N_U, 2]), ALU.mult,
+        )
+
+        gauss_products = held.tile([P, N_F, N_U, N_F], F32)
+        nc.vector.tensor_tensor(
+            gauss_products[:],
+            whiten[:].rearrange("g r a -> g a r").unsqueeze(3).to_broadcast([P, N_F, N_U, N_F]),
+            whiten[:].unsqueeze(1).to_broadcast([P, N_F, N_U, N_F]),
+            ALU.mult,
+        )
+        gauss_rows_psum = psum.tile([K, n_gauss], F32)
+        nc.tensor.transpose(gauss_rows_psum[:], gauss_products[:].rearrange("g a r b -> g (a r b)"), identity[:])
+        gauss_rows = held.tile([K, n_gauss], F32)
+        nc.vector.tensor_copy(gauss_rows[:], gauss_rows_psum[:])
+
+        for blk in range(n_blocks):
+            twice_sigma = psum.tile([P, n_gauss], F32, name=f"twice_sigma{blk}")
+            nc.tensor.matmul(
+                twice_sigma[:], pixel_products[:, blk * P : (blk + 1) * P], gauss_rows[:], start=True, stop=True
+            )
+            falloff = held.tile([P, n_gauss], F32, name=f"falloff{blk}")
+            nc.scalar.activation(falloff[:], twice_sigma[:], ACT.Exp, scale=-0.5)
+            nc.vector.tensor_tensor(windows[blk][:].indirect(offsets[:]), falloff[:], opacity_all[:], ALU.mult)
+            nc.sync.dma_start(out[blk * P : (blk + 1) * P, :], windows[blk][:])

@@ -13,7 +13,7 @@ IMAGE_W, IMAGE_H = 32, 16
 N_F = 4
 N_U = 2
 K = N_F * N_U * N_F
-STAGE_ROWS = 64
+N_PARAMS = 5
 
 FLOPS = 2 * K * 512 * 128
 
@@ -29,8 +29,6 @@ def tile_gaussianbasis_kernel(tc, base, xyz_raw, cholesky_raw, opacity, px, py, 
         held = ctx.enter_context(tc.tile_pool(name="held", bufs=1))
         psum = ctx.enter_context(tc.psum_pool(name="psum", bufs=1))
 
-        stage = held.tile([STAGE_ROWS, n_gauss], F32)
-        nc.vector.memset(stage[:], 0.0)
         second = held.tile([K, n_pixels], F32)
         nc.gpsimd.memset(second[:], 1.0)
         identity = held.tile([P, P], F32)
@@ -41,33 +39,34 @@ def tile_gaussianbasis_kernel(tc, base, xyz_raw, cholesky_raw, opacity, px, py, 
         whiten = held.tile([P, N_U, N_F], F32)
         nc.vector.memset(whiten[:], 0.0)
 
+        stage = held.tile([N_PARAMS, n_gauss], F32)
         nc.sync.dma_start(stage[0:2, :], xyz_raw)
-        nc.scalar.dma_start(stage[2:4, :], cholesky_raw[0:2, :])
+        nc.sync.dma_start(stage[2:4, :], cholesky_raw[0:2, :])
         nc.sync.dma_start(stage[4:5, :], cholesky_raw[2:3, :])
 
         px_row = px.rearrange("c o -> (c o)")
         py_row = py.rearrange("c o -> (c o)")
         rows_per_a = N_U * N_F
-        nc.scalar.dma_start(first[2 * rows_per_a : 3 * rows_per_a, :], px_row.partition_broadcast(rows_per_a))
+        nc.sync.dma_start(first[2 * rows_per_a : 3 * rows_per_a, :], px_row.partition_broadcast(rows_per_a))
         nc.sync.dma_start(first[3 * rows_per_a : 4 * rows_per_a, :], py_row.partition_broadcast(rows_per_a))
-        nc.scalar.dma_start(second[2::N_F, :], px_row.partition_broadcast(K // N_F))
+        nc.sync.dma_start(second[2::N_F, :], px_row.partition_broadcast(K // N_F))
         nc.sync.dma_start(second[3::N_F, :], py_row.partition_broadcast(K // N_F))
 
         offsets = held.tile([P, n_gauss // 16], U16)
         nc.sync.dma_start(offsets[:], offs)
         opacity_all = held.tile([P, n_gauss], F32)
-        nc.scalar.dma_start(opacity_all[:], opacity.rearrange("o n -> (o n)").partition_broadcast(P))
+        nc.sync.dma_start(opacity_all[:], opacity.rearrange("o n -> (o n)").partition_broadcast(P))
 
         windows = [held.tile([P, n_slots], F32, name=f"window{blk}") for blk in range(n_blocks)]
         for blk in range(n_blocks):
-            queue = nc.sync if blk % 2 == 0 else nc.scalar
+            queue = nc.sync if blk == 0 else nc.scalar
             queue.dma_start(windows[blk][:], base[blk * P : (blk + 1) * P, :])
 
         pixel_products = held.tile([K, n_pixels], F32)
         nc.gpsimd.tensor_tensor(pixel_products[:], first[:], second[:], ALU.mult)
 
-        params = psum.tile([P, STAGE_ROWS], F32)
-        nc.tensor.transpose(params[:], stage[:], identity[0:STAGE_ROWS, 0:STAGE_ROWS])
+        params = psum.tile([P, N_PARAMS], F32)
+        nc.tensor.matmul(params[:], stage[:], identity[0:N_PARAMS, 0:N_PARAMS], start=True, stop=True)
 
         tanh_xy = held.tile([P, 2], F32)
         nc.scalar.activation(tanh_xy[:], params[:, 0:2], ACT.Tanh)

@@ -59,8 +59,7 @@ def tile_gaussianbasis_kernel(tc, base, xyz_raw, cholesky_raw, opacity, px, py, 
 
         windows = [held.tile([P, n_slots], F32, name=f"window{blk}") for blk in range(n_blocks)]
         for blk in range(n_blocks):
-            queue = nc.sync if blk == 0 else nc.scalar
-            queue.dma_start(windows[blk][:], base[blk * P : (blk + 1) * P, :])
+            nc.sync.dma_start(windows[blk][:], base[blk * P : (blk + 1) * P, :])
 
         pixel_products = held.tile([K, n_pixels], F32)
         nc.gpsimd.tensor_tensor(pixel_products[:], first[:], second[:], ALU.mult)

@@ -67,15 +67,6 @@ def tile_gaussianbasis_kernel(tc, base, xyz_raw, cholesky_raw, opacity, px, py, 
         params = psum.tile([P, N_PARAMS], F32)
         nc.tensor.matmul(params[:], stage[:], identity[0:N_PARAMS, 0:N_PARAMS], start=True, stop=True)
 
-        tanh_xy = held.tile([P, 2], F32)
-        nc.scalar.activation(tanh_xy[:], params[:, 0:2], ACT.Tanh)
-        minus_centre = held.tile([P, 2], F32)
-        for axis, size in enumerate((IMAGE_W, IMAGE_H)):
-            nc.vector.tensor_scalar(
-                minus_centre[:, axis : axis + 1], tanh_xy[:, axis : axis + 1],
-                -0.5 * size, -0.5 * (size - 1), ALU.mult, ALU.add,
-            )
-
         whiten_flat = whiten[:].rearrange("g r a -> g (r a)")
         minus_l = held.tile([P, 2], F32)
         nc.vector.tensor_scalar(minus_l[:], params[:, 2:5:2], 0.5, -1.0, ALU.add, ALU.mult)
@@ -84,6 +75,16 @@ def tile_gaussianbasis_kernel(tc, base, xyz_raw, cholesky_raw, opacity, px, py, 
             whiten_flat[:, N_F + 2 : N_F + 3], params[:, 3:4],
             whiten_flat[:, 2:3], whiten_flat[:, N_F + 3 : N_F + 4], ALU.mult, ALU.mult,
         )
+
+        tanh_xy = held.tile([P, 2], F32)
+        nc.scalar.activation(tanh_xy[:], params[:, 0:2], ACT.Tanh)
+        minus_centre = held.tile([P, 2], F32)
+        for axis, size in enumerate((IMAGE_W, IMAGE_H)):
+            nc.scalar.activation(
+                minus_centre[:, axis : axis + 1], tanh_xy[:, axis : axis + 1],
+                ACT.Copy, bias=-0.5 * (size - 1), scale=-0.5 * size,
+            )
+
         nc.vector.tensor_tensor(
             whiten[:, :, 0:2], whiten[:, :, 2:4],
             minus_centre[:].unsqueeze(1).to_broadcast([P, N_U, 2]), ALU.mult,

@@ -1,6 +1,5 @@
 from contextlib import ExitStack
 
-import concourse.masks as masks
 import concourse.mybir as mybir
 
 F32 = mybir.dt.float32
@@ -13,7 +12,8 @@ IMAGE_W, IMAGE_H = 32, 16
 N_F = 4
 N_U = 2
 K = N_F * N_U * N_F
-N_PARAMS = 5
+SQUARE = 32
+assert K == SQUARE
 
 FLOPS = 2 * K * 512 * 128
 
@@ -23,23 +23,25 @@ def tile_gaussianbasis_kernel(tc, base, xyz_raw, cholesky_raw, opacity, px, py, 
     n_pixels, n_slots = base.shape
     n_gauss = opacity.shape[1]
     n_blocks = n_pixels // P
-    assert n_gauss == P and n_pixels % P == 0
+    n_groups = n_gauss // SQUARE
+    assert n_pixels % P == 0 and n_gauss % SQUARE == 0
 
     with ExitStack() as ctx:
         held = ctx.enter_context(tc.tile_pool(name="held", bufs=1))
         psum = ctx.enter_context(tc.psum_pool(name="psum", bufs=1))
 
+        stage = held.tile([P, n_gauss], F32, align_bytes=64)
+        nc.vector.memset(stage[:], 0.0)
         second = held.tile([K, n_pixels], F32)
         nc.gpsimd.memset(second[:], 1.0)
-        identity = held.tile([P, P], F32)
-        masks.make_identity(nc, identity[:])
         first = held.tile([K, n_pixels], F32)
         ones_rows = 2 * N_U * N_F
         nc.vector.memset(first[0:ones_rows, :], 1.0)
-        whiten = held.tile([P, N_U, N_F], F32)
+        whiten = held.tile([SQUARE, n_groups, N_U, N_F], F32)
         nc.vector.memset(whiten[:], 0.0)
+        gauss_products = held.tile([P, n_groups * K], F32, align_bytes=64)
+        nc.vector.memset(gauss_products[:], 0.0)
 
-        stage = held.tile([N_PARAMS, n_gauss], F32)
         nc.sync.dma_start(stage[0:2, :], xyz_raw)
         nc.sync.dma_start(stage[2:4, :], cholesky_raw[0:2, :])
         nc.sync.dma_start(stage[4:5, :], cholesky_raw[2:3, :])
@@ -64,48 +66,46 @@ def tile_gaussianbasis_kernel(tc, base, xyz_raw, cholesky_raw, opacity, px, py, 
         pixel_products = held.tile([K, n_pixels], F32)
         nc.gpsimd.tensor_tensor(pixel_products[:], first[:], second[:], ALU.mult)
 
-        params = psum.tile([P, N_PARAMS], F32)
-        nc.tensor.matmul(params[:], stage[:], identity[0:N_PARAMS, 0:N_PARAMS], start=True, stop=True)
+        flipped = held.tile([P, n_gauss], F32, align_bytes=64)
+        nc.vector.transpose(flipped[:], stage[:])
+        params = flipped[0:SQUARE, :].rearrange("i (c k) -> i c k", k=SQUARE)
 
-        whiten_flat = whiten[:].rearrange("g r a -> g (r a)")
-        minus_l = held.tile([P, 2], F32)
-        nc.vector.tensor_scalar(minus_l[:], params[:, 2:5:2], 0.5, -1.0, ALU.add, ALU.mult)
-        nc.vector.reciprocal(whiten_flat[:, 2 : 2 * N_F : N_F + 1], minus_l[:])
-        nc.vector.tensor_scalar(
-            whiten_flat[:, N_F + 2 : N_F + 3], params[:, 3:4],
-            whiten_flat[:, 2:3], whiten_flat[:, N_F + 3 : N_F + 4], ALU.mult, ALU.mult,
-        )
-
-        tanh_xy = held.tile([P, 2], F32)
-        nc.scalar.activation(tanh_xy[:], params[:, 0:2], ACT.Tanh)
-        minus_centre = held.tile([P, 2], F32)
+        tanh_xy = held.tile([SQUARE, n_groups, 2], F32)
+        nc.scalar.activation(tanh_xy[:], params[:, :, 0:2], ACT.Tanh)
+        minus_centre = held.tile([SQUARE, n_groups, 2], F32)
         for axis, size in enumerate((IMAGE_W, IMAGE_H)):
-            nc.scalar.activation(
-                minus_centre[:, axis : axis + 1], tanh_xy[:, axis : axis + 1],
-                ACT.Copy, bias=-0.5 * (size - 1), scale=-0.5 * size,
+            nc.vector.tensor_scalar(
+                minus_centre[:, :, axis : axis + 1], tanh_xy[:, :, axis : axis + 1],
+                -0.5 * size, -0.5 * (size - 1), ALU.mult, ALU.add,
             )
 
+        minus_l = held.tile([SQUARE, n_groups, 2], F32)
+        nc.vector.tensor_scalar(minus_l[:], params[:, :, 2:5:2], 0.5, -1.0, ALU.add, ALU.mult)
+        whiten_flat = whiten[:].rearrange("i c r a -> i c (r a)")
+        nc.vector.reciprocal(whiten_flat[:, :, 2 : 2 * N_F : N_F + 1], minus_l[:])
+        l2_w00 = held.tile([SQUARE, n_groups, 1], F32)
+        nc.vector.tensor_tensor(l2_w00[:], params[:, :, 3:4], whiten[:, :, 0, 2:3], ALU.mult)
+        nc.vector.tensor_tensor(whiten[:, :, 1, 2:3], l2_w00[:], whiten[:, :, 1, 3:4], ALU.mult)
         nc.vector.tensor_tensor(
-            whiten[:, :, 0:2], whiten[:, :, 2:4],
-            minus_centre[:].unsqueeze(1).to_broadcast([P, N_U, 2]), ALU.mult,
+            whiten[:, :, :, 0:2], whiten[:, :, :, 2:4],
+            minus_centre[:].unsqueeze(2).to_broadcast([SQUARE, n_groups, N_U, 2]), ALU.mult,
         )
 
-        gauss_products = held.tile([P, N_F, N_U, N_F], F32)
-        nc.vector.tensor_tensor(
-            gauss_products[:],
-            whiten[:].rearrange("g r a -> g a r").unsqueeze(3).to_broadcast([P, N_F, N_U, N_F]),
-            whiten[:].unsqueeze(1).to_broadcast([P, N_F, N_U, N_F]),
-            ALU.mult,
-        )
-        gauss_rows_psum = psum.tile([K, n_gauss], F32)
-        nc.tensor.transpose(gauss_rows_psum[:], gauss_products[:].rearrange("g a r b -> g (a r b)"), identity[:])
-        gauss_rows = held.tile([K, n_gauss], F32)
-        nc.vector.tensor_copy(gauss_rows[:], gauss_rows_psum[:])
+        products = gauss_products[0:SQUARE, :].rearrange("i (c a r b) -> i c a r b", a=N_F, r=N_U, b=N_F)
+        for r in range(N_U):
+            nc.vector.tensor_tensor(
+                products[:, :, :, r, :],
+                whiten[:, :, r, :].unsqueeze(3).to_broadcast([SQUARE, n_groups, N_F, N_F]),
+                whiten[:, :, r, :].unsqueeze(2).to_broadcast([SQUARE, n_groups, N_F, N_F]),
+                ALU.mult,
+            )
+        gauss_rows = held.tile([P, n_gauss], F32, align_bytes=64)
+        nc.vector.transpose(gauss_rows[:], gauss_products[:])
 
         for blk in range(n_blocks):
             twice_sigma = psum.tile([P, n_gauss], F32, name=f"twice_sigma{blk}")
             nc.tensor.matmul(
-                twice_sigma[:], pixel_products[:, blk * P : (blk + 1) * P], gauss_rows[:], start=True, stop=True
+                twice_sigma[:], pixel_products[:, blk * P : (blk + 1) * P], gauss_rows[0:K, :], start=True, stop=True
             )
             falloff = held.tile([P, n_gauss], F32, name=f"falloff{blk}")
             nc.scalar.activation(falloff[:], twice_sigma[:], ACT.Exp, scale=-0.5)

@@ -1,5 +1,6 @@
 from contextlib import ExitStack
 
+import concourse.masks as masks
 import concourse.mybir as mybir
 
 F32 = mybir.dt.float32
@@ -12,8 +13,7 @@ IMAGE_W, IMAGE_H = 32, 16
 N_F = 4
 N_U = 2
 K = N_F * N_U * N_F
-SQUARE = 32
-assert K == SQUARE
+N_PARAMS = 5
 
 FLOPS = 2 * K * 512 * 128
 
@@ -23,25 +23,23 @@ def tile_gaussianbasis_kernel(tc, base, xyz_raw, cholesky_raw, opacity, px, py, 
     n_pixels, n_slots = base.shape
     n_gauss = opacity.shape[1]
     n_blocks = n_pixels // P
-    n_groups = n_gauss // SQUARE
-    assert n_pixels % P == 0 and n_gauss % SQUARE == 0
+    assert n_gauss == P and n_pixels % P == 0
 
     with ExitStack() as ctx:
         held = ctx.enter_context(tc.tile_pool(name="held", bufs=1))
         psum = ctx.enter_context(tc.psum_pool(name="psum", bufs=1))
 
-        stage = held.tile([P, n_gauss], F32, align_bytes=64)
-        nc.vector.memset(stage[:], 0.0)
         second = held.tile([K, n_pixels], F32)
         nc.gpsimd.memset(second[:], 1.0)
+        identity = held.tile([P, P], F32)
+        masks.make_identity(nc, identity[:])
         first = held.tile([K, n_pixels], F32)
         ones_rows = 2 * N_U * N_F
         nc.vector.memset(first[0:ones_rows, :], 1.0)
-        whiten = held.tile([SQUARE, n_groups, N_U, N_F], F32)
+        whiten = held.tile([P, N_U, N_F], F32)
         nc.vector.memset(whiten[:], 0.0)
-        gauss_products = held.tile([P, n_groups * K], F32, align_bytes=64)
-        nc.vector.memset(gauss_products[:], 0.0)
 
+        stage = held.tile([N_PARAMS, n_gauss], F32)
         nc.sync.dma_start(stage[0:2, :], xyz_raw)
         nc.sync.dma_start(stage[2:4, :], cholesky_raw[0:2, :])
         nc.sync.dma_start(stage[4:5, :], cholesky_raw[2:3, :])
@@ -64,48 +62,51 @@ def tile_gaussianbasis_kernel(tc, base, xyz_raw, cholesky_raw, opacity, px, py, 
             nc.sync.dma_start(windows[blk][:], base[blk * P : (blk + 1) * P, :])
 
         pixel_products = held.tile([K, n_pixels], F32)
-        nc.gpsimd.tensor_tensor(pixel_products[:], first[:], second[:], ALU.mult)
+        for blk in range(n_blocks):
+            cols = slice(blk * P, (blk + 1) * P)
+            nc.gpsimd.tensor_tensor(pixel_products[:, cols], first[:, cols], second[:, cols], ALU.mult)
 
-        flipped = held.tile([P, n_gauss], F32, align_bytes=64)
-        nc.vector.transpose(flipped[:], stage[:])
-        params = flipped[0:SQUARE, :].rearrange("i (c k) -> i c k", k=SQUARE)
+        params = psum.tile([P, N_PARAMS], F32)
+        nc.tensor.matmul(params[:], stage[:], identity[0:N_PARAMS, 0:N_PARAMS], start=True, stop=True)
 
-        tanh_xy = held.tile([SQUARE, n_groups, 2], F32)
-        nc.scalar.activation(tanh_xy[:], params[:, :, 0:2], ACT.Tanh)
-        minus_centre = held.tile([SQUARE, n_groups, 2], F32)
+        tanh_xy = held.tile([P, 2], F32)
+        nc.scalar.activation(tanh_xy[:], params[:, 0:2], ACT.Tanh)
+        minus_centre = held.tile([P, 2], F32)
         for axis, size in enumerate((IMAGE_W, IMAGE_H)):
             nc.vector.tensor_scalar(
-                minus_centre[:, :, axis : axis + 1], tanh_xy[:, :, axis : axis + 1],
+                minus_centre[:, axis : axis + 1], tanh_xy[:, axis : axis + 1],
                 -0.5 * size, -0.5 * (size - 1), ALU.mult, ALU.add,
             )
 
-        minus_l = held.tile([SQUARE, n_groups, 2], F32)
-        nc.vector.tensor_scalar(minus_l[:], params[:, :, 2:5:2], 0.5, -1.0, ALU.add, ALU.mult)
-        whiten_flat = whiten[:].rearrange("i c r a -> i c (r a)")
-        nc.vector.reciprocal(whiten_flat[:, :, 2 : 2 * N_F : N_F + 1], minus_l[:])
-        l2_w00 = held.tile([SQUARE, n_groups, 1], F32)
-        nc.vector.tensor_tensor(l2_w00[:], params[:, :, 3:4], whiten[:, :, 0, 2:3], ALU.mult)
-        nc.vector.tensor_tensor(whiten[:, :, 1, 2:3], l2_w00[:], whiten[:, :, 1, 3:4], ALU.mult)
+        whiten_flat = whiten[:].rearrange("g r a -> g (r a)")
+        minus_l = held.tile([P, 2], F32)
+        nc.vector.tensor_scalar(minus_l[:], params[:, 2:5:2], 0.5, -1.0, ALU.add, ALU.mult)
+        nc.vector.reciprocal(whiten_flat[:, 2 : 2 * N_F : N_F + 1], minus_l[:])
+        nc.vector.tensor_scalar(
+            whiten_flat[:, N_F + 2 : N_F + 3], params[:, 3:4],
+            whiten_flat[:, 2:3], whiten_flat[:, N_F + 3 : N_F + 4], ALU.mult, ALU.mult,
+        )
         nc.vector.tensor_tensor(
-            whiten[:, :, :, 0:2], whiten[:, :, :, 2:4],
-            minus_centre[:].unsqueeze(2).to_broadcast([SQUARE, n_groups, N_U, 2]), ALU.mult,
+            whiten[:, :, 0:2], whiten[:, :, 2:4],
+            minus_centre[:].unsqueeze(1).to_broadcast([P, N_U, 2]), ALU.mult,
         )
 
-        products = gauss_products[0:SQUARE, :].rearrange("i (c a r b) -> i c a r b", a=N_F, r=N_U, b=N_F)
-        for r in range(N_U):
-            nc.vector.tensor_tensor(
-                products[:, :, :, r, :],
-                whiten[:, :, r, :].unsqueeze(3).to_broadcast([SQUARE, n_groups, N_F, N_F]),
-                whiten[:, :, r, :].unsqueeze(2).to_broadcast([SQUARE, n_groups, N_F, N_F]),
-                ALU.mult,
-            )
-        gauss_rows = held.tile([P, n_gauss], F32, align_bytes=64)
-        nc.vector.transpose(gauss_rows[:], gauss_products[:])
+        gauss_products = held.tile([P, N_F, N_U, N_F], F32)
+        nc.vector.tensor_tensor(
+            gauss_products[:],
+            whiten[:].rearrange("g r a -> g a r").unsqueeze(3).to_broadcast([P, N_F, N_U, N_F]),
+            whiten[:].unsqueeze(1).to_broadcast([P, N_F, N_U, N_F]),
+            ALU.mult,
+        )
+        gauss_rows_psum = psum.tile([K, n_gauss], F32)
+        nc.tensor.transpose(gauss_rows_psum[:], gauss_products[:].rearrange("g a r b -> g (a r b)"), identity[:])
+        gauss_rows = held.tile([K, n_gauss], F32)
+        nc.vector.tensor_copy(gauss_rows[:], gauss_rows_psum[:])
 
         for blk in range(n_blocks):
             twice_sigma = psum.tile([P, n_gauss], F32, name=f"twice_sigma{blk}")
             nc.tensor.matmul(
-                twice_sigma[:], pixel_products[:, blk * P : (blk + 1) * P], gauss_rows[0:K, :], start=True, stop=True
+                twice_sigma[:], pixel_products[:, blk * P : (blk + 1) * P], gauss_rows[:], start=True, stop=True
             )
             falloff = held.tile([P, n_gauss], F32, name=f"falloff{blk}")
             nc.scalar.activation(falloff[:], twice_sigma[:], ACT.Exp, scale=-0.5)

@@ -11,9 +11,8 @@ ACT = mybir.ActivationFunctionType
 P = 128
 IMAGE_W, IMAGE_H = 32, 16
 N_F = 4
-N_U = 2
-K = N_F * N_U * N_F
-N_PARAMS = 5
+N_V = 2
+K = N_F * N_V * N_F
 
 FLOPS = 2 * K * 512 * 128
 
@@ -34,19 +33,22 @@ def tile_gaussianbasis_kernel(tc, base, xyz_raw, cholesky_raw, opacity, px, py, 
         identity = held.tile([P, P], F32)
         masks.make_identity(nc, identity[:])
         first = held.tile([K, n_pixels], F32)
-        ones_rows = 2 * N_U * N_F
+        ones_rows = 2 * N_V * N_F
         nc.vector.memset(first[0:ones_rows, :], 1.0)
-        whiten = held.tile([P, N_U, N_F], F32)
-        nc.vector.memset(whiten[:], 0.0)
+        forms = held.tile([P, N_V, N_F], F32)
+        nc.vector.memset(forms[:], 0.0)
+        minus_half_size_a = held.tile([P, N_V, 2], F32)
+        nc.vector.memset(minus_half_size_a[:], 0.0)
 
-        stage = held.tile([N_PARAMS, n_gauss], F32)
-        nc.sync.dma_start(stage[0:2, :], xyz_raw)
-        nc.sync.dma_start(stage[2:4, :], cholesky_raw[0:2, :])
-        nc.sync.dma_start(stage[4:5, :], cholesky_raw[2:3, :])
+        xy_raw = held.tile([P, 2], F32)
+        chol = held.tile([P, 3], F32)
+        with nc.allow_non_contiguous_dma(reason="640 single values, one Gaussian to a partition"):
+            nc.sync.dma_start(xy_raw[:], xyz_raw.rearrange("r g -> g r"))
+            nc.sync.dma_start(chol[:], cholesky_raw.rearrange("r g -> g r"))
 
         px_row = px.rearrange("c o -> (c o)")
         py_row = py.rearrange("c o -> (c o)")
-        rows_per_a = N_U * N_F
+        rows_per_a = N_V * N_F
         nc.sync.dma_start(first[2 * rows_per_a : 3 * rows_per_a, :], px_row.partition_broadcast(rows_per_a))
         nc.sync.dma_start(first[3 * rows_per_a : 4 * rows_per_a, :], py_row.partition_broadcast(rows_per_a))
         nc.sync.dma_start(second[2::N_F, :], px_row.partition_broadcast(K // N_F))
@@ -66,40 +68,46 @@ def tile_gaussianbasis_kernel(tc, base, xyz_raw, cholesky_raw, opacity, px, py, 
             cols = slice(blk * P, (blk + 1) * P)
             nc.gpsimd.tensor_tensor(pixel_products[:, cols], first[:, cols], second[:, cols], ALU.mult)
 
-        params = psum.tile([P, N_PARAMS], F32)
-        nc.tensor.matmul(params[:], stage[:], identity[0:N_PARAMS, 0:N_PARAMS], start=True, stop=True)
+        chol_diag = chol[:, 0:3:2]
+        chol_off = chol[:, 1:2]
 
         tanh_xy = held.tile([P, 2], F32)
-        nc.scalar.activation(tanh_xy[:], params[:, 0:2], ACT.Tanh)
-        minus_centre = held.tile([P, 2], F32)
+        nc.scalar.activation(tanh_xy[:], xy_raw[:], ACT.Tanh)
+        squares = held.tile([P, 2], F32)
+        nc.scalar.activation(squares[:], chol_diag, ACT.Square, bias=0.5)
+
+        scaled_flat = minus_half_size_a[:].rearrange("g r c -> g (r c)")
+        nc.vector.tensor_scalar(scaled_flat[:, 0:1], chol_off, 0.5 * IMAGE_W, None, ALU.mult)
+        nc.vector.tensor_scalar(scaled_flat[:, 1:2], chol[:, 0:1], 0.5, -0.5 * IMAGE_H, ALU.add, ALU.mult)
+        nc.vector.tensor_scalar(scaled_flat[:, 2:3], chol[:, 2:3], 0.5, -0.5 * IMAGE_W, ALU.add, ALU.mult)
+        forms_flat = forms[:].rearrange("g r a -> g (r a)")
+        nc.vector.tensor_scalar(forms_flat[:, 3 : N_F + 3 : 3], chol_diag, 0.5, None, ALU.add)
+        nc.vector.tensor_scalar(forms_flat[:, 2:3], chol_off, -1.0, None, ALU.mult)
+
         for axis, size in enumerate((IMAGE_W, IMAGE_H)):
-            nc.vector.tensor_scalar(
-                minus_centre[:, axis : axis + 1], tanh_xy[:, axis : axis + 1],
-                -0.5 * size, -0.5 * (size - 1), ALU.mult, ALU.add,
+            nc.vector.scalar_tensor_tensor(
+                forms[:, :, axis], tanh_xy[:, axis : axis + 1].to_broadcast([P, N_V]), (size - 1) / size,
+                minus_half_size_a[:, :, axis], ALU.add, ALU.mult,
             )
 
-        whiten_flat = whiten[:].rearrange("g r a -> g (r a)")
-        minus_l = held.tile([P, 2], F32)
-        nc.vector.tensor_scalar(minus_l[:], params[:, 2:5:2], 0.5, -1.0, ALU.add, ALU.mult)
-        nc.vector.reciprocal(whiten_flat[:, 2 : 2 * N_F : N_F + 1], minus_l[:])
-        nc.vector.tensor_scalar(
-            whiten_flat[:, N_F + 2 : N_F + 3], params[:, 3:4],
-            whiten_flat[:, 2:3], whiten_flat[:, N_F + 3 : N_F + 4], ALU.mult, ALU.mult,
-        )
-        nc.vector.tensor_tensor(
-            whiten[:, :, 0:2], whiten[:, :, 2:4],
-            minus_centre[:].unsqueeze(1).to_broadcast([P, N_U, 2]), ALU.mult,
-        )
-
-        gauss_products = held.tile([P, N_F, N_U, N_F], F32)
+        gauss_products = held.tile([P, N_F, N_V, N_F], F32)
         nc.vector.tensor_tensor(
             gauss_products[:],
-            whiten[:].rearrange("g r a -> g a r").unsqueeze(3).to_broadcast([P, N_F, N_U, N_F]),
-            whiten[:].unsqueeze(1).to_broadcast([P, N_F, N_U, N_F]),
+            forms[:].rearrange("g r a -> g a r").unsqueeze(3).to_broadcast([P, N_F, N_V, N_F]),
+            forms[:].unsqueeze(1).to_broadcast([P, N_F, N_V, N_F]),
             ALU.mult,
         )
+
+        inverse_squares = held.tile([P, 2], F32)
+        nc.vector.reciprocal(inverse_squares[:], squares[:])
+        gauss_coefficients = held.tile([P, K], F32)
+        nc.vector.tensor_scalar(
+            gauss_coefficients[:], gauss_products[:].rearrange("g a r b -> g (a r b)"),
+            inverse_squares[:, 0:1], inverse_squares[:, 1:2], ALU.mult, ALU.mult,
+        )
+
         gauss_rows_psum = psum.tile([K, n_gauss], F32)
-        nc.tensor.transpose(gauss_rows_psum[:], gauss_products[:].rearrange("g a r b -> g (a r b)"), identity[:])
+        nc.tensor.transpose(gauss_rows_psum[:], gauss_coefficients[:], identity[:])
         gauss_rows = held.tile([K, n_gauss], F32)
         nc.vector.tensor_copy(gauss_rows[:], gauss_rows_psum[:])
 

@@ -64,9 +64,10 @@ def tile_gaussianbasis_kernel(tc, base, xyz_raw, cholesky_raw, opacity, px, py, 
             nc.sync.dma_start(windows[blk][:], base[blk * P : (blk + 1) * P, :])
 
         pixel_products = held.tile([K, n_pixels], F32)
-        for blk in range(n_blocks):
+
+        def multiply_pixel_rows(blk):
             cols = slice(blk * P, (blk + 1) * P)
-            nc.gpsimd.tensor_tensor(pixel_products[:, cols], first[:, cols], second[:, cols], ALU.mult)
+            nc.vector.tensor_tensor(pixel_products[:, cols], first[:, cols], second[:, cols], ALU.mult)
 
         chol_diag = chol[:, 0:3:2]
         chol_off = chol[:, 1:2]
@@ -108,8 +109,11 @@ def tile_gaussianbasis_kernel(tc, base, xyz_raw, cholesky_raw, opacity, px, py, 
 
         gauss_rows_psum = psum.tile([K, n_gauss], F32)
         nc.tensor.transpose(gauss_rows_psum[:], gauss_coefficients[:], identity[:])
+        multiply_pixel_rows(0)
         gauss_rows = held.tile([K, n_gauss], F32)
         nc.vector.tensor_copy(gauss_rows[:], gauss_rows_psum[:])
+        for blk in range(1, n_blocks):
+            multiply_pixel_rows(blk)
 
         for blk in range(n_blocks):
             twice_sigma = psum.tile([P, n_gauss], F32, name=f"twice_sigma{blk}")

@@ -54,13 +54,13 @@ def tile_gaussianbasis_kernel(tc, base, xyz_raw, cholesky_raw, opacity, px, py, 
         nc.sync.dma_start(second[2::N_F, :], px_row.partition_broadcast(K // N_F))
         nc.sync.dma_start(second[3::N_F, :], py_row.partition_broadcast(K // N_F))
 
-        offsets = held.tile([P, n_gauss // 16], U16)
-        nc.sync.dma_start(offsets[:], offs)
         opacity_all = held.tile([P, n_gauss], F32)
         nc.sync.dma_start(opacity_all[:], opacity.rearrange("o n -> (o n)").partition_broadcast(P))
-
         windows = [held.tile([P, n_slots], F32, name=f"window{blk}") for blk in range(n_blocks)]
-        for blk in range(n_blocks):
+        nc.sync.dma_start(windows[0][:], base[0:P, :])
+        offsets = held.tile([P, n_gauss // 16], U16)
+        nc.sync.dma_start(offsets[:], offs)
+        for blk in range(1, n_blocks):
             nc.sync.dma_start(windows[blk][:], base[blk * P : (blk + 1) * P, :])
 
         pixel_products = held.tile([K, n_pixels], F32)

@@ -29,7 +29,7 @@ def tile_gaussianbasis_kernel(tc, base, xyz_raw, cholesky_raw, opacity, px, py, 
         psum = ctx.enter_context(tc.psum_pool(name="psum", bufs=1))
 
         second = held.tile([K, n_pixels], F32)
-        nc.gpsimd.memset(second[:], 1.0)
+        nc.vector.memset(second[:], 1.0)
         identity = held.tile([P, P], F32)
         masks.make_identity(nc, identity[:])
         first = held.tile([K, n_pixels], F32)

@@ -43,8 +43,8 @@ def tile_gaussianbasis_kernel(tc, base, xyz_raw, cholesky_raw, opacity, px, py, 
         xy_raw = held.tile([P, 2], F32)
         chol = held.tile([P, 3], F32)
         with nc.allow_non_contiguous_dma(reason="640 single values, one Gaussian to a partition"):
-            nc.sync.dma_start(xy_raw[:], xyz_raw.rearrange("r g -> g r"))
             nc.sync.dma_start(chol[:], cholesky_raw.rearrange("r g -> g r"))
+            nc.sync.dma_start(xy_raw[:], xyz_raw.rearrange("r g -> g r"))
 
         px_row = px.rearrange("c o -> (c o)")
         py_row = py.rearrange("c o -> (c o)")

@@ -36,9 +36,14 @@ def tile_gaussianbasis_kernel(tc, base, xyz_raw, cholesky_raw, opacity, px, py, 
         ones_rows = 2 * N_V * N_F
         nc.vector.memset(first[0:ones_rows, :], 1.0)
         forms = held.tile([P, N_V, N_F], F32)
-        nc.vector.memset(forms[:], 0.0)
-        minus_half_size_a = held.tile([P, N_V, 2], F32)
-        nc.vector.memset(minus_half_size_a[:], 0.0)
+        half_size_a = held.tile([P, N_V, 2], F32)
+        nc.vector.memset(half_size_a[:], 0.0)
+        diag_scales = held.tile([P, 2], F32)
+        nc.vector.memset(diag_scales[:, 0:1], -0.5 * IMAGE_H)
+        nc.vector.memset(diag_scales[:, 1:2], 0.5 * IMAGE_W)
+        per_half_size = held.tile([P, 2], F32)
+        nc.vector.memset(per_half_size[:, 0:1], 2.0 / IMAGE_W)
+        nc.vector.memset(per_half_size[:, 1:2], 2.0 / IMAGE_H)
 
         xy_raw = held.tile([P, 2], F32)
         chol = held.tile([P, 3], F32)
@@ -72,43 +77,38 @@ def tile_gaussianbasis_kernel(tc, base, xyz_raw, cholesky_raw, opacity, px, py, 
         chol_diag = chol[:, 0:3:2]
         chol_off = chol[:, 1:2]
 
-        tanh_xy = held.tile([P, 2], F32)
-        nc.scalar.activation(tanh_xy[:], xy_raw[:], ACT.Tanh)
         squares = held.tile([P, 2], F32)
         nc.scalar.activation(squares[:], chol_diag, ACT.Square, bias=0.5)
+        minus_tanh = held.tile([P, 2], F32)
+        nc.scalar.activation(minus_tanh[:], xy_raw[:], ACT.Tanh, scale=-1.0)
 
-        scaled_flat = minus_half_size_a[:].rearrange("g r c -> g (r c)")
-        nc.vector.tensor_scalar(scaled_flat[:, 0:1], chol_off, 0.5 * IMAGE_W, None, ALU.mult)
-        nc.vector.tensor_scalar(scaled_flat[:, 1:2], chol[:, 0:1], 0.5, -0.5 * IMAGE_H, ALU.add, ALU.mult)
-        nc.vector.tensor_scalar(scaled_flat[:, 2:3], chol[:, 2:3], 0.5, -0.5 * IMAGE_W, ALU.add, ALU.mult)
-        forms_flat = forms[:].rearrange("g r a -> g (r a)")
-        nc.vector.tensor_scalar(forms_flat[:, 3 : N_F + 3 : 3], chol_diag, 0.5, None, ALU.add)
-        nc.vector.tensor_scalar(forms_flat[:, 2:3], chol_off, -1.0, None, ALU.mult)
-
+        factors_flat = half_size_a[:].rearrange("g r c -> g (r c)")
+        nc.vector.scalar_tensor_tensor(
+            factors_flat[:, 1:3], chol_diag, 0.5, diag_scales[:], ALU.add, ALU.mult
+        )
+        nc.vector.tensor_scalar(factors_flat[:, 0:1], chol_off, 0.5 * IMAGE_W, None, ALU.mult)
+        nc.vector.tensor_tensor(
+            forms[:, :, 2:4], half_size_a[:], per_half_size[:].unsqueeze(1).to_broadcast([P, N_V, 2]), ALU.mult
+        )
         for axis, size in enumerate((IMAGE_W, IMAGE_H)):
             nc.vector.scalar_tensor_tensor(
-                forms[:, :, axis], tanh_xy[:, axis : axis + 1].to_broadcast([P, N_V]), (size - 1) / size,
-                minus_half_size_a[:, :, axis], ALU.add, ALU.mult,
+                forms[:, :, axis], minus_tanh[:, axis : axis + 1].to_broadcast([P, N_V]), -(size - 1) / size,
+                half_size_a[:, :, axis], ALU.add, ALU.mult,
             )
-
-        gauss_products = held.tile([P, N_F, N_V, N_F], F32)
-        nc.vector.tensor_tensor(
-            gauss_products[:],
-            forms[:].rearrange("g r a -> g a r").unsqueeze(3).to_broadcast([P, N_F, N_V, N_F]),
-            forms[:].unsqueeze(1).to_broadcast([P, N_F, N_V, N_F]),
-            ALU.mult,
-        )
 
         inverse_squares = held.tile([P, 2], F32)
         nc.vector.reciprocal(inverse_squares[:], squares[:])
-        gauss_coefficients = held.tile([P, K], F32)
-        nc.vector.tensor_scalar(
-            gauss_coefficients[:], gauss_products[:].rearrange("g a r b -> g (a r b)"),
-            inverse_squares[:, 0:1], inverse_squares[:, 1:2], ALU.mult, ALU.mult,
-        )
+        inverse_det = held.tile([P, 1], F32)
+        nc.vector.tensor_tensor(inverse_det[:], inverse_squares[:, 0:1], inverse_squares[:, 1:2], ALU.mult)
+        gauss_coefficients = held.tile([P, N_F, N_V, N_F], F32)
+        for r in range(N_V):
+            nc.vector.scalar_tensor_tensor(
+                gauss_coefficients[:, :, r, :], forms[:, r, :].unsqueeze(2).to_broadcast([P, N_F, N_F]),
+                inverse_det[:], forms[:, r, :].unsqueeze(1).to_broadcast([P, N_F, N_F]), ALU.mult, ALU.mult,
+            )
 
         gauss_rows_psum = psum.tile([K, n_gauss], F32)
-        nc.tensor.transpose(gauss_rows_psum[:], gauss_coefficients[:], identity[:])
+        nc.tensor.transpose(gauss_rows_psum[:], gauss_coefficients[:].rearrange("g a r b -> g (a r b)"), identity[:])
         multiply_pixel_rows(0)
         gauss_rows = held.tile([K, n_gauss], F32)
         nc.vector.tensor_copy(gauss_rows[:], gauss_rows_psum[:])

from contextlib import ExitStack

import concourse.masks as masks
import concourse.mybir as mybir

F32 = mybir.dt.float32
U16 = mybir.dt.uint16
ALU = mybir.AluOpType
ACT = mybir.ActivationFunctionType

P = 128
IMAGE_W, IMAGE_H = 32, 16
N_F = 4
N_V = 2
K = N_F * N_V * N_F

FLOPS = 2 * K * 512 * 128


def tile_gaussianbasis_kernel(tc, base, xyz_raw, cholesky_raw, opacity, px, py, offs, out):
    nc = tc.nc
    n_pixels, n_slots = base.shape
    n_gauss = opacity.shape[1]
    n_blocks = n_pixels // P
    assert n_gauss == P and n_pixels % P == 0

    with ExitStack() as ctx:
        held = ctx.enter_context(tc.tile_pool(name="held", bufs=1))
        psum = ctx.enter_context(tc.psum_pool(name="psum", bufs=1))

        second = held.tile([K, n_pixels], F32)
        nc.vector.memset(second[:], 1.0)
        identity = held.tile([P, P], F32)
        masks.make_identity(nc, identity[:])
        first = held.tile([K, n_pixels], F32)
        ones_rows = 2 * N_V * N_F
        nc.vector.memset(first[0:ones_rows, :], 1.0)
        forms = held.tile([P, N_V, N_F], F32)
        half_size_a = held.tile([P, N_V, 2], F32)
        nc.vector.memset(half_size_a[:], 0.0)
        diag_scales = held.tile([P, 2], F32)
        nc.vector.memset(diag_scales[:, 0:1], -0.5 * IMAGE_H)
        nc.vector.memset(diag_scales[:, 1:2], 0.5 * IMAGE_W)
        per_half_size = held.tile([P, 2], F32)
        nc.vector.memset(per_half_size[:, 0:1], 2.0 / IMAGE_W)
        nc.vector.memset(per_half_size[:, 1:2], 2.0 / IMAGE_H)

        xy_raw = held.tile([P, 2], F32)
        chol = held.tile([P, 3], F32)
        with nc.allow_non_contiguous_dma(reason="640 single values, one Gaussian to a partition"):
            nc.sync.dma_start(chol[:], cholesky_raw.rearrange("r g -> g r"))
            nc.sync.dma_start(xy_raw[:], xyz_raw.rearrange("r g -> g r"))

        px_row = px.rearrange("c o -> (c o)")
        py_row = py.rearrange("c o -> (c o)")
        rows_per_a = N_V * N_F
        nc.sync.dma_start(first[2 * rows_per_a : 3 * rows_per_a, :], px_row.partition_broadcast(rows_per_a))
        nc.sync.dma_start(first[3 * rows_per_a : 4 * rows_per_a, :], py_row.partition_broadcast(rows_per_a))
        nc.sync.dma_start(second[2::N_F, :], px_row.partition_broadcast(K // N_F))
        nc.sync.dma_start(second[3::N_F, :], py_row.partition_broadcast(K // N_F))

        opacity_all = held.tile([P, n_gauss], F32)
        nc.sync.dma_start(opacity_all[:], opacity.rearrange("o n -> (o n)").partition_broadcast(P))
        windows = [held.tile([P, n_slots], F32, name=f"window{blk}") for blk in range(n_blocks)]
        nc.sync.dma_start(windows[0][:], base[0:P, :])
        offsets = held.tile([P, n_gauss // 16], U16)
        nc.sync.dma_start(offsets[:], offs)
        for blk in range(1, n_blocks):
            nc.sync.dma_start(windows[blk][:], base[blk * P : (blk + 1) * P, :])

        pixel_products = held.tile([K, n_pixels], F32)

        def multiply_pixel_rows(blk):
            cols = slice(blk * P, (blk + 1) * P)
            nc.vector.tensor_tensor(pixel_products[:, cols], first[:, cols], second[:, cols], ALU.mult)

        chol_diag = chol[:, 0:3:2]
        chol_off = chol[:, 1:2]

        squares = held.tile([P, 2], F32)
        nc.scalar.activation(squares[:], chol_diag, ACT.Square, bias=0.5)
        minus_tanh = held.tile([P, 2], F32)
        nc.scalar.activation(minus_tanh[:], xy_raw[:], ACT.Tanh, scale=-1.0)

        factors_flat = half_size_a[:].rearrange("g r c -> g (r c)")
        nc.vector.scalar_tensor_tensor(
            factors_flat[:, 1:3], chol_diag, 0.5, diag_scales[:], ALU.add, ALU.mult
        )
        nc.vector.tensor_scalar(factors_flat[:, 0:1], chol_off, 0.5 * IMAGE_W, None, ALU.mult)
        nc.vector.tensor_tensor(
            forms[:, :, 2:4], half_size_a[:], per_half_size[:].unsqueeze(1).to_broadcast([P, N_V, 2]), ALU.mult
        )
        for axis, size in enumerate((IMAGE_W, IMAGE_H)):
            nc.vector.scalar_tensor_tensor(
                forms[:, :, axis], minus_tanh[:, axis : axis + 1].to_broadcast([P, N_V]), -(size - 1) / size,
                half_size_a[:, :, axis], ALU.add, ALU.mult,
            )

        inverse_squares = held.tile([P, 2], F32)
        nc.vector.reciprocal(inverse_squares[:], squares[:])
        inverse_det = held.tile([P, 1], F32)
        nc.vector.tensor_tensor(inverse_det[:], inverse_squares[:, 0:1], inverse_squares[:, 1:2], ALU.mult)
        gauss_coefficients = held.tile([P, N_F, N_V, N_F], F32)
        for r in range(N_V):
            nc.vector.scalar_tensor_tensor(
                gauss_coefficients[:, :, r, :], forms[:, r, :].unsqueeze(2).to_broadcast([P, N_F, N_F]),
                inverse_det[:], forms[:, r, :].unsqueeze(1).to_broadcast([P, N_F, N_F]), ALU.mult, ALU.mult,
            )

        gauss_rows_psum = psum.tile([K, n_gauss], F32)
        nc.tensor.transpose(gauss_rows_psum[:], gauss_coefficients[:].rearrange("g a r b -> g (a r b)"), identity[:])
        multiply_pixel_rows(0)
        gauss_rows = held.tile([K, n_gauss], F32)
        nc.vector.tensor_copy(gauss_rows[:], gauss_rows_psum[:])
        for blk in range(1, n_blocks):
            multiply_pixel_rows(blk)

        for blk in range(n_blocks):
            twice_sigma = psum.tile([P, n_gauss], F32, name=f"twice_sigma{blk}")
            nc.tensor.matmul(
                twice_sigma[:], pixel_products[:, blk * P : (blk + 1) * P], gauss_rows[:], start=True, stop=True
            )
            falloff = held.tile([P, n_gauss], F32, name=f"falloff{blk}")
            nc.scalar.activation(falloff[:], twice_sigma[:], ACT.Exp, scale=-0.5)
            nc.vector.tensor_tensor(windows[blk][:].indirect(offsets[:]), falloff[:], opacity_all[:], ALU.mult)
            nc.sync.dma_start(out[blk * P : (blk + 1) * P, :], windows[blk][:])
